import numpy as np
import ml_dtypes


def mxq(x, axis, fmt="e4m3"):
    dtype, down = {"e4m3": (ml_dtypes.float8_e4m3fn, 7), "e5m2": (ml_dtypes.float8_e5m2, 14)}[fmt]
    v = np.moveaxis(np.asarray(x, np.float32).astype(ml_dtypes.bfloat16).astype(np.float64), axis, -1)
    blocks = v.reshape(v.shape[:-1] + (-1, 32))
    amax = np.abs(blocks).max(-1, keepdims=True)
    byte = np.maximum(np.where(amax > 0, np.frexp(amax)[1] - 1 + 127, 0) - down, 1)
    scale = np.exp2(byte - 127.0)
    codes = (blocks / scale).astype(np.float32).astype(dtype).astype(np.float64)
    return np.moveaxis((codes * scale).reshape(v.shape), -1, axis)


WIDE = False


def mx_kscale(k):
    if not WIDE:
        return np.ones(k)
    levels = np.array([10, -10, 5, -5, 0])
    a = np.random.permutation(np.resize(levels, k // 512 * 4)).reshape(k // 512, 4)
    idx = np.arange(k)
    return np.exp2(a[idx // 512, idx % 128 // 32])


BF16 = ml_dtypes.bfloat16


def bf(x):
    return np.asarray(x, np.float32).astype(BF16)


def f64(x):
    return np.asarray(x).astype(np.float64)


E2M1 = np.array([0.0, 0.5, 1.0, 1.5, 2.0, 3.0, 4.0, 6.0, -0.0, -0.5, -1.0, -1.5, -2.0, -3.0, -4.0, -6.0])


def pack_weight(w, fmt):
    k, n = w.shape
    w = f64(bf(w)).reshape(k // 32, 32, n)
    amax = np.abs(w).max(1)
    if fmt == "e4m3":
        byte = np.frexp(amax)[1] - 1 + 127 - 7
    else:
        mant, ex = np.frexp(amax / 6.0)
        byte = np.where(mant > 0.5, ex, ex - 1) + 127
    byte = np.clip(np.where(amax > 0, byte, 1), 1, 254)
    scaled = (w * np.exp2(127.0 - byte)[:, None, :]).reshape(k, n).astype(np.float32)
    by_word = np.ascontiguousarray(scaled.reshape(k // 512, 128, 4, n).transpose(0, 1, 3, 2))
    if fmt == "e4m3":
        words = by_word.astype(ml_dtypes.float8_e4m3fn).view(np.uint8)
    else:
        c = by_word.astype(ml_dtypes.float4_e2m1fn).view(np.uint8) & 0xF
        words = c[..., 0::2] | (c[..., 1::2] << 4)
    return np.ascontiguousarray(words), np.ascontiguousarray(byte.astype(np.uint8).reshape(k // 512, 16, n))


def unpack_weight(words, scales, fmt):
    g, p, n, _ = words.shape
    if fmt == "e4m3":
        vals = np.ascontiguousarray(words).view(ml_dtypes.float8_e4m3fn).astype(np.float64)
    else:
        nib = np.empty((g, p, n, 4), np.uint8)
        nib[..., 0::2] = words & 0xF
        nib[..., 1::2] = words >> 4
        vals = E2M1[nib]
    vals = vals * np.repeat(np.exp2(scales.astype(np.float64) - 127.0), 8, axis=1)[..., None]
    return vals.transpose(0, 1, 3, 2).reshape(g * 512, n)


B, E, D = 256, 2048, 2048
FMT = "e4m3"


def hard_sigmoid(z):
    return np.clip(z / 6.0 + 0.5, 0.0, 1.0)


def setup_inputs():
    s = mx_kscale(E)
    t = mx_kscale(D)
    x = bf(np.random.standard_normal((B, E)) * s)
    state_x = bf(np.random.standard_normal((B, E)) * s)
    time_mix_r = bf(np.random.uniform(0.0, 1.0, (1, E)))
    w_r = np.random.standard_normal((D, E)) * 3.5 / np.sqrt(E) / s[None, :]
    wr_words, wr_scales = pack_weight(np.ascontiguousarray(w_r.T), FMT)
    wkv_num = bf((0.5 + 0.5 * np.random.standard_normal((B, D))) * t)
    wkv_den = bf(0.5 + 1.5 * np.random.uniform(0.0, 1.0, (B, D)))
    w_o = np.random.standard_normal((E, D)) * 2.0 / np.sqrt(D) / t[None, :]
    wo_words, wo_scales = pack_weight(np.ascontiguousarray(w_o.T), FMT)
    return {
        "x": x,
        "state_x": state_x,
        "time_mix_r": time_mix_r,
        "W_receptance_words": wr_words,
        "W_receptance_scales": wr_scales,
        "wkv_num": wkv_num,
        "wkv_den": wkv_den,
        "W_output_words": wo_words,
        "W_output_scales": wo_scales,
    }


def reference(x, state_x, time_mix_r, W_receptance_words, W_receptance_scales, wkv_num, wkv_den, W_output_words, W_output_scales):
    x, state_x, mr = f64(x), f64(state_x), f64(time_mix_r)
    xr = x * mr + state_x * (1.0 - mr)
    r = hard_sigmoid(mxq(xr, 1, "e4m3") @ unpack_weight(W_receptance_words, W_receptance_scales, FMT))
    h = r * f64(wkv_num) / f64(wkv_den)
    return mxq(h, 1, "e4m3") @ unpack_weight(W_output_words, W_output_scales, FMT)

@@ -1,0 +1,274 @@
+from contextlib import ExitStack
+
+import concourse.mybir as mybir
+from concourse.masks import make_identity
+
+F32 = mybir.dt.float32
+BF16 = mybir.dt.bfloat16
+I32 = mybir.dt.int32
+U32 = mybir.dt.uint32
+U8 = mybir.dt.uint8
+FP8X4 = mybir.dt.float8_e4m3fn_x4
+ACT = mybir.ActivationFunctionType
+ALU = mybir.AluOpType
+
+P = 128
+ROWS = 256
+ROW_TILES = ROWS // P
+WIDTH = 2048
+PACK = 4
+K_PASS = P * PACK
+GROUPS = WIDTH // K_PASS
+N_TILE = 512
+COL_TILES = WIDTH // N_TILE
+PAIR = 2
+WORDS_PASS = K_PASS // PAIR
+
+FLOPS = 2 * 2 * ROWS * WIDTH * WIDTH
+
+
+def tile_rwkv_timemix_for_quant_pb_kernel(
+    tc,
+    x,
+    state_x,
+    time_mix_r,
+    W_receptance_words,
+    W_receptance_scales,
+    wkv_num,
+    wkv_den,
+    W_output_words,
+    W_output_scales,
+    out,
+):
+    nc = tc.nc
+    with ExitStack() as ctx:
+        keep = ctx.enter_context(tc.tile_pool(name="keep", bufs=1))
+        work = ctx.enter_context(tc.tile_pool(name="work", bufs=2))
+        psum = ctx.enter_context(tc.psum_pool(name="psum", bufs=8))
+        ctx.enter_context(tc.manual_schedule())
+
+        x_sb = keep.tile([P, ROW_TILES, WIDTH], BF16)
+        sx_sb = keep.tile([P, ROW_TILES, WIDTH], BF16)
+        num_sb = keep.tile([P, ROW_TILES, WIDTH], BF16)
+        den_sb = keep.tile([P, ROW_TILES, WIDTH], BF16)
+        h_sb = keep.tile([P, ROW_TILES, WIDTH], BF16)
+        gate = keep.tile([P, ROW_TILES, WIDTH], F32)
+        out_sb = keep.tile([P, ROW_TILES, WIDTH], F32)
+        wr_words = keep.tile([P, GROUPS, WIDTH], U32, align_bytes=64)
+        wo_words = keep.tile([P, GROUPS, WIDTH], U32, align_bytes=64)
+        wr_planes = keep.tile([P, WIDTH], U8, align_bytes=64)
+        wo_planes = keep.tile([P, WIDTH], U8, align_bytes=64)
+        xr_codes = keep.tile([P, GROUPS, ROWS], U32, align_bytes=64)
+        xr_scales = keep.tile([P, GROUPS, ROWS], U8, align_bytes=64)
+        h_codes = keep.tile([P, GROUPS, ROWS], U32, align_bytes=64)
+        h_scales = keep.tile([P, GROUPS, ROWS], U8, align_bytes=64)
+        ident = keep.tile([P, P], F32)
+        mix_bf = keep.tile([P, GROUPS, PACK], BF16)
+        mix = keep.tile([P, GROUPS * PACK], F32)
+        one_minus_mix = keep.tile([P, GROUPS * PACK], F32)
+        warm = keep.tile([P, 1], F32)
+
+        nc.scalar.dma_start(
+            out=mix_bf[:],
+            in_=time_mix_r.rearrange("o (g p t) -> p (o g) t", g=GROUPS, p=P, t=PACK),
+        )
+        nc.vector.memset(wr_planes[:].bitcast(I32), 0)
+        nc.vector.memset(wo_planes[:].bitcast(I32), 0)
+        nc.vector.memset(warm[:], 1.0)
+        nc.scalar.activation(out=warm[:], in_=warm[:], func=ACT.Abs_reciprocal_sqrt)
+        make_identity(nc, ident[:])
+        mix_flat = mix_bf[:].rearrange("p g t -> p (g t)")
+        nc.vector.tensor_copy(out=mix[:], in_=mix_flat)
+        nc.vector.tensor_scalar(
+            out=one_minus_mix[:], in0=mix_flat, scalar1=-1.0, scalar2=1.0, op0=ALU.mult, op1=ALU.add
+        )
+
+        def load_rows(dst, src, first, count):
+            nc.sync.dma_start(
+                out=dst[:, :, first : first + count],
+                in_=src.rearrange("(r p) e -> p r e", p=P)[:, :, first : first + count],
+            )
+
+        def load_planes(planes, scales):
+            for quad in range(4):
+                nc.sync.dma_start(
+                    out=planes[32 * quad : 32 * quad + 16, :].bitcast(I32),
+                    in_=scales[:, 4 * quad : 4 * quad + 4, :].bitcast(I32),
+                )
+
+        def load_words(dst, words, c):
+            first = c * N_TILE
+            for g in range(GROUPS):
+                packed = words[g].rearrange("p n t -> p (n t)")
+                nc.sync.dma_start(
+                    out=dst[:, g, first : first + N_TILE].bitcast(I32),
+                    in_=packed[:, PACK * first : PACK * (first + N_TILE)].bitcast(I32),
+                )
+
+        for first in range(0, WIDTH, WIDTH // 2):
+            load_rows(sx_sb, state_x, first, WIDTH // 2)
+            load_rows(x_sb, x, first, WIDTH // 2)
+        load_rows(den_sb, wkv_den, 0, WIDTH)
+        load_planes(wr_planes, W_receptance_scales)
+        load_words(wr_words, W_receptance_words, 0)
+        load_rows(num_sb, wkv_num, 0, WIDTH)
+        for c in range(1, COL_TILES):
+            load_words(wr_words, W_receptance_words, c)
+        load_planes(wo_planes, W_output_scales)
+        for c in range(COL_TILES):
+            load_words(wo_words, W_output_words, c)
+
+        def transpose_pass(src, g, name):
+            bank = psum.tile([P, PAIR, ROWS], F32, name=name, tag="bank")
+            for r in range(ROW_TILES):
+                words = src[:, r, :].bitcast(F32)
+                for u in range(PAIR):
+                    nc.tensor.transpose(
+                        bank[:, u, r * P : (r + 1) * P],
+                        words[:, WORDS_PASS * g + u : WORDS_PASS * (g + 1) : PAIR],
+                        ident[:],
+                    )
+            return bank
+
+        def halves_of(bank):
+            return bank[:].bitcast(BF16).rearrange("p u (r e) -> p u r e", e=PAIR)
+
+        def mix_pass(g):
+            sx_t = transpose_pass(sx_sb, g, "sx_t")
+            x_t = transpose_pass(x_sb, g, "x_t")
+            kept = work.tile([P, PACK, ROWS], F32)
+            mixed = work.tile([P, PACK, ROWS], BF16)
+            for t in range(PACK):
+                u, e = divmod(t, PAIR)
+                col = PACK * g + t
+                nc.scalar.activation(
+                    out=kept[:, t, :],
+                    in_=halves_of(sx_t)[:, u, :, e],
+                    func=ACT.Copy,
+                    scale=one_minus_mix[:, col : col + 1],
+                )
+                nc.vector.scalar_tensor_tensor(
+                    out=mixed[:, t, :],
+                    in0=halves_of(x_t)[:, u, :, e],
+                    scalar=mix[:, col : col + 1],
+                    in1=kept[:, t, :],
+                    op0=ALU.mult,
+                    op1=ALU.add,
+                )
+            return mixed
+
+        def group_planes(mixed):
+            grouped = work.tile([P, ROWS, PACK], BF16, name="xr_grouped", align_bytes=64)
+            nc.vector.tensor_copy(out=grouped[:], in_=mixed[:].rearrange("p t r -> p r t"))
+            return grouped
+
+        def quantise(grouped, codes, scales, g):
+            nc.vector.quantize_mx(
+                out=codes[:, g, :].bitcast(FP8X4),
+                scales=scales[:, g, :],
+                in_=grouped[:].rearrange("p r t -> p (r t)"),
+            )
+
+        def accumulators(name):
+            return [psum.tile([P, N_TILE], F32, name="%s%d" % (name, r), tag="bank") for r in range(ROW_TILES)]
+
+        def product(acc, codes, scales, w_words, w_planes, c, g):
+            first = c * N_TILE
+            for r in range(ROW_TILES):
+                nc.tensor.matmul_mx(
+                    out=acc[r][:],
+                    lhsT=codes[:, g, r * P : (r + 1) * P].bitcast(FP8X4),
+                    lhsT_scale=scales[:, g, r * P : (r + 1) * P],
+                    rhs=w_words[:, g, first : first + N_TILE].bitcast(FP8X4),
+                    rhs_scale=w_planes[PACK * g : P, first : first + N_TILE],
+                    start=(g == 0),
+                    stop=(g == GROUPS - 1),
+                )
+
+        def gate_on_scalar(c):
+            cols = slice(c * N_TILE, (c + 1) * N_TILE)
+            nc.scalar.activation(
+                out=gate[:, :, cols], in_=den_sb[:, :, cols], func=ACT.Abs_reciprocal_sqrt, scale=6.0
+            )
+            nc.scalar.activation(out=gate[:, :, cols], in_=gate[:, :, cols], func=ACT.Square)
+
+        def gate_on_vector(c):
+            cols = slice(c * N_TILE, (c + 1) * N_TILE)
+            nc.vector.tensor_mul(out=gate[:, :, cols], in0=num_sb[:, :, cols], in1=gate[:, :, cols])
+
+        def gated(z, c):
+            cols = slice(c * N_TILE, (c + 1) * N_TILE)
+            for r in range(ROW_TILES):
+                ramp = work.tile([P, N_TILE], F32, bufs=4)
+                nc.scalar.activation(out=ramp[:], in_=z[r][:], func=ACT.Relu, bias=3.0)
+                nc.vector.scalar_tensor_tensor(
+                    out=h_sb[:, r, cols],
+                    in0=ramp[:],
+                    scalar=6.0,
+                    in1=gate[:, r, cols],
+                    op0=ALU.min,
+                    op1=ALU.mult,
+                )
+
+        def group_h(g):
+            h_t = transpose_pass(h_sb, g, "h_t")
+            grouped = work.tile([P, ROWS, PACK], BF16, name="h_grouped", align_bytes=64)
+            nc.vector.tensor_copy(
+                out=grouped[:].rearrange("p r t -> p (r t)").bitcast(F32).rearrange("p (r u) -> p r u", u=PAIR),
+                in_=h_t[:].rearrange("p u r -> p r u"),
+            )
+            return grouped
+
+        out_rows = out.rearrange("(r p) e -> p r e", p=P)
+
+        def leave(y, c):
+            cols = slice(c * N_TILE, (c + 1) * N_TILE)
+            nc.scalar.copy(out=out_sb[:, 0, cols], in_=y[0][:])
+            nc.vector.tensor_copy(out=out_sb[:, 1, cols], in_=y[1][:])
+            for r in range(ROW_TILES):
+                nc.sync.dma_start(out=out_rows[:, r, cols], in_=out_sb[:, r, cols])
+
+        mixed_of = {}
+        grouped_of = {}
+        for g in range(GROUPS + 2):
+            if g < GROUPS:
+                mixed_of[g] = mix_pass(g)
+            if 1 <= g <= GROUPS:
+                grouped_of[g - 1] = group_planes(mixed_of[g - 1])
+            if g >= 2:
+                quantise(grouped_of[g - 2], xr_codes, xr_scales, g - 2)
+
+        gate_on_scalar(0)
+        gate_on_scalar(1)
+        gate_on_vector(0)
+        for c in range(COL_TILES):
+            z = accumulators("z")
+            for g in range(GROUPS):
+                product(z, xr_codes, xr_scales, wr_words, wr_planes, c, g)
+            if c >= 1:
+                h_grouped = group_h(c - 1)
+            gated(z, c)
+            if c >= 1:
+                quantise(h_grouped, h_codes, h_scales, c - 1)
+            if c + 1 < COL_TILES:
+                gate_on_vector(c + 1)
+            if c + 2 < COL_TILES:
+                gate_on_scalar(c + 2)
+
+        y_0 = accumulators("y")
+        for g in range(GROUPS - 1):
+            product(y_0, h_codes, h_scales, wo_words, wo_planes, 0, g)
+        h_grouped = group_h(COL_TILES - 1)
+        quantise(h_grouped, h_codes, h_scales, COL_TILES - 1)
+        y_1 = accumulators("y")
+        for g in range(GROUPS - 1):
+            product(y_1, h_codes, h_scales, wo_words, wo_planes, 1, g)
+        product(y_0, h_codes, h_scales, wo_words, wo_planes, 0, GROUPS - 1)
+        leave(y_0, 0)
+        product(y_1, h_codes, h_scales, wo_words, wo_planes, 1, GROUPS - 1)
+        leave(y_1, 1)
+        for c in range(2, COL_TILES):
+            y = accumulators("y")
+            for g in range(GROUPS):
+                product(y, h_codes, h_scales, wo_words, wo_planes, c, g)
+            leave(y, c)

@@ -21,6 +21,7 @@ K_PASS = P * PACK
 GROUPS = WIDTH // K_PASS
 N_TILE = 512
 COL_TILES = WIDTH // N_TILE
+EARLY = 2
 PAIR = 2
 WORDS_PASS = K_PASS // PAIR
 
@@ -96,13 +97,14 @@ def tile_rwkv_timemix_for_quant_pb_kernel(
                     in_=scales[:, 4 * quad : 4 * quad + 4, :].bitcast(I32),
                 )
 
-        def load_words(dst, words, c):
-            first = c * N_TILE
+        def load_words(dst, words, first_tile, tiles):
+            first = first_tile * N_TILE
+            count = tiles * N_TILE
             for g in range(GROUPS):
                 packed = words[g].rearrange("p n t -> p (n t)")
                 nc.sync.dma_start(
-                    out=dst[:, g, first : first + N_TILE].bitcast(I32),
-                    in_=packed[:, PACK * first : PACK * (first + N_TILE)].bitcast(I32),
+                    out=dst[:, g, first : first + count].bitcast(I32),
+                    in_=packed[:, PACK * first : PACK * (first + count)].bitcast(I32),
                 )
 
         for first in range(0, WIDTH, WIDTH // 2):
@@ -110,13 +112,14 @@ def tile_rwkv_timemix_for_quant_pb_kernel(
             load_rows(x_sb, x, first, WIDTH // 2)
         load_rows(den_sb, wkv_den, 0, WIDTH)
         load_planes(wr_planes, W_receptance_scales)
-        load_words(wr_words, W_receptance_words, 0)
+        load_words(wr_words, W_receptance_words, 0, EARLY)
         load_rows(num_sb, wkv_num, 0, WIDTH)
-        for c in range(1, COL_TILES):
-            load_words(wr_words, W_receptance_words, c)
+        for c in range(EARLY, COL_TILES):
+            load_words(wr_words, W_receptance_words, c, 1)
         load_planes(wo_planes, W_output_scales)
-        for c in range(COL_TILES):
-            load_words(wo_words, W_output_words, c)
+        load_words(wo_words, W_output_words, 0, EARLY)
+        for c in range(EARLY, COL_TILES):
+            load_words(wo_words, W_output_words, c, 1)
 
         def transpose_pass(src, g, name):
             bank = psum.tile([P, PAIR, ROWS], F32, name=name, tag="bank")
@@ -159,7 +162,10 @@ def tile_rwkv_timemix_for_quant_pb_kernel(
 
         def group_planes(mixed):
             grouped = work.tile([P, ROWS, PACK], BF16, name="xr_grouped", align_bytes=64)
-            nc.vector.tensor_copy(out=grouped[:], in_=mixed[:].rearrange("p t r -> p r t"))
+            nc.vector.tensor_copy(
+                out=grouped[:].rearrange("p (c i) t -> p c t i", i=4),
+                in_=mixed[:].rearrange("p t (c i) -> p c t i", i=4),
+            )
             return grouped
 
         def quantise(grouped, codes, scales, g):
@@ -185,14 +191,17 @@ def tile_rwkv_timemix_for_quant_pb_kernel(
                     stop=(g == GROUPS - 1),
                 )
 
-        def gate_on_scalar(c):
+        def gate_root(c):
             cols = slice(c * N_TILE, (c + 1) * N_TILE)
             nc.scalar.activation(
                 out=gate[:, :, cols], in_=den_sb[:, :, cols], func=ACT.Abs_reciprocal_sqrt, scale=6.0
             )
+
+        def gate_square(c):
+            cols = slice(c * N_TILE, (c + 1) * N_TILE)
             nc.scalar.activation(out=gate[:, :, cols], in_=gate[:, :, cols], func=ACT.Square)
 
-        def gate_on_vector(c):
+        def gate_times_num(c):
             cols = slice(c * N_TILE, (c + 1) * N_TILE)
             nc.vector.tensor_mul(out=gate[:, :, cols], in0=num_sb[:, :, cols], in1=gate[:, :, cols])
 
@@ -238,37 +247,47 @@ def tile_rwkv_timemix_for_quant_pb_kernel(
             if g >= 2:
                 quantise(grouped_of[g - 2], xr_codes, xr_scales, g - 2)
 
-        gate_on_scalar(0)
-        gate_on_scalar(1)
-        gate_on_vector(0)
+        z_of = {}
+        for c in range(EARLY):
+            z_of[c] = accumulators("z")
+        for g in range(GROUPS):
+            for c in range(EARLY):
+                product(z_of[c], xr_codes, xr_scales, wr_words, wr_planes, c, g)
+        gate_root(0)
+        gate_root(1)
+        gate_square(0)
+        gate_square(1)
+        gate_times_num(0)
         for c in range(COL_TILES):
-            z = accumulators("z")
-            for g in range(GROUPS):
-                product(z, xr_codes, xr_scales, wr_words, wr_planes, c, g)
+            if c >= EARLY:
+                z_of[c] = accumulators("z")
+                for g in range(GROUPS):
+                    product(z_of[c], xr_codes, xr_scales, wr_words, wr_planes, c, g)
             if c >= 1:
                 h_grouped = group_h(c - 1)
-            gated(z, c)
+            if c + 2 < COL_TILES:
+                gate_root(c + 2)
+            gated(z_of[c], c)
             if c >= 1:
                 quantise(h_grouped, h_codes, h_scales, c - 1)
             if c + 1 < COL_TILES:
-                gate_on_vector(c + 1)
+                gate_times_num(c + 1)
             if c + 2 < COL_TILES:
-                gate_on_scalar(c + 2)
+                gate_square(c + 2)
 
-        y_0 = accumulators("y")
-        for g in range(GROUPS - 1):
-            product(y_0, h_codes, h_scales, wo_words, wo_planes, 0, g)
-        h_grouped = group_h(COL_TILES - 1)
-        quantise(h_grouped, h_codes, h_scales, COL_TILES - 1)
-        y_1 = accumulators("y")
-        for g in range(GROUPS - 1):
-            product(y_1, h_codes, h_scales, wo_words, wo_planes, 1, g)
-        product(y_0, h_codes, h_scales, wo_words, wo_planes, 0, GROUPS - 1)
-        leave(y_0, 0)
-        product(y_1, h_codes, h_scales, wo_words, wo_planes, 1, GROUPS - 1)
-        leave(y_1, 1)
-        for c in range(2, COL_TILES):
-            y = accumulators("y")
+        y_of = {}
+        for c in range(EARLY):
+            y_of[c] = accumulators("y")
+        for g in range(GROUPS):
+            if g == GROUPS - 2:
+                h_grouped = group_h(COL_TILES - 1)
+                quantise(h_grouped, h_codes, h_scales, COL_TILES - 1)
+            for c in range(EARLY):
+                product(y_of[c], h_codes, h_scales, wo_words, wo_planes, c, g)
+        for c in range(EARLY):
+            leave(y_of[c], c)
+        for c in range(EARLY, COL_TILES):
+            y_of[c] = accumulators("y")
             for g in range(GROUPS):
-                product(y, h_codes, h_scales, wo_words, wo_planes, c, g)
-            leave(y, c)
+                product(y_of[c], h_codes, h_scales, wo_words, wo_planes, c, g)
+            leave(y_of[c], c)

@@ -25,6 +25,8 @@ EARLY = 2
 PAIR = 2
 WORDS_PASS = K_PASS // PAIR
 
+RAMPS = 4
+LATE = 3
 FLOPS = 2 * 2 * ROWS * WIDTH * WIDTH
 
 
@@ -45,7 +47,7 @@ def tile_rwkv_timemix_for_quant_pb_kernel(
     with ExitStack() as ctx:
         keep = ctx.enter_context(tc.tile_pool(name="keep", bufs=1))
         work = ctx.enter_context(tc.tile_pool(name="work", bufs=2))
-        psum = ctx.enter_context(tc.psum_pool(name="psum", bufs=8))
+        psum = ctx.enter_context(tc.psum_pool(name="psum", bufs=1))
         ctx.enter_context(tc.manual_schedule())
 
         x_sb = keep.tile([P, ROW_TILES, WIDTH], BF16)
@@ -68,6 +70,9 @@ def tile_rwkv_timemix_for_quant_pb_kernel(
         mix = keep.tile([P, GROUPS * PACK], F32)
         one_minus_mix = keep.tile([P, GROUPS * PACK], F32)
         warm = keep.tile([P, 1], F32)
+
+        def bank(b, shape, name):
+            return psum.tile(shape, F32, name=name, tag="bank%d" % b)
 
         nc.scalar.dma_start(
             out=mix_bf[:],
@@ -97,68 +102,92 @@ def tile_rwkv_timemix_for_quant_pb_kernel(
                     in_=scales[:, 4 * quad : 4 * quad + 4, :].bitcast(I32),
                 )
 
-        def load_words(dst, words, first_tile, tiles):
+        def load_words(dst, words, first_tile, tiles, groups):
             first = first_tile * N_TILE
             count = tiles * N_TILE
-            for g in range(GROUPS):
+            for g in groups:
                 packed = words[g].rearrange("p n t -> p (n t)")
                 nc.sync.dma_start(
                     out=dst[:, g, first : first + count].bitcast(I32),
                     in_=packed[:, PACK * first : PACK * (first + count)].bitcast(I32),
                 )
 
-        for first in range(0, WIDTH, WIDTH // 2):
-            load_rows(sx_sb, state_x, first, WIDTH // 2)
-            load_rows(x_sb, x, first, WIDTH // 2)
-        load_rows(den_sb, wkv_den, 0, WIDTH)
+        HALF = WIDTH // 2
+        for g in range(2):
+            load_rows(sx_sb, state_x, g * K_PASS, K_PASS)
+            load_rows(x_sb, x, g * K_PASS, K_PASS)
+        load_rows(sx_sb, state_x, HALF, HALF)
+        load_rows(x_sb, x, HALF, HALF)
         load_planes(wr_planes, W_receptance_scales)
-        load_words(wr_words, W_receptance_words, 0, EARLY)
-        load_rows(num_sb, wkv_num, 0, WIDTH)
-        for c in range(EARLY, COL_TILES):
-            load_words(wr_words, W_receptance_words, c, 1)
+        load_words(wr_words, W_receptance_words, 0, EARLY, (0,))
+        load_rows(den_sb, wkv_den, 0, HALF)
+        load_words(wr_words, W_receptance_words, 0, EARLY, (1,))
+        load_rows(den_sb, wkv_den, HALF, HALF)
         load_planes(wo_planes, W_output_scales)
-        load_words(wo_words, W_output_words, 0, EARLY)
-        for c in range(EARLY, COL_TILES):
-            load_words(wo_words, W_output_words, c, 1)
+        load_words(wr_words, W_receptance_words, 0, EARLY, (2, 3))
+        load_rows(num_sb, wkv_num, 0, HALF)
+        load_words(wr_words, W_receptance_words, 2, 1, range(GROUPS))
+        load_rows(num_sb, wkv_num, HALF, HALF)
+        load_words(wr_words, W_receptance_words, 3, 1, range(GROUPS))
+        for c in range(LATE):
+            load_words(wo_words, W_output_words, c, 1, (0,))
+        load_words(wo_words, W_output_words, 0, LATE, range(1, GROUPS))
+        load_words(wo_words, W_output_words, LATE, 1, range(GROUPS))
 
-        def transpose_pass(src, g, name):
-            bank = psum.tile([P, PAIR, ROWS], F32, name=name, tag="bank")
-            for r in range(ROW_TILES):
+        def transpose_pass(src, g, rows, b, name):
+            t_bank = bank(b, [P, PAIR, len(rows) * P], name)
+            for i, r in enumerate(rows):
                 words = src[:, r, :].bitcast(F32)
                 for u in range(PAIR):
                     nc.tensor.transpose(
-                        bank[:, u, r * P : (r + 1) * P],
+                        t_bank[:, u, i * P : (i + 1) * P],
                         words[:, WORDS_PASS * g + u : WORDS_PASS * (g + 1) : PAIR],
                         ident[:],
                     )
-            return bank
+            return t_bank
 
-        def halves_of(bank):
-            return bank[:].bitcast(BF16).rearrange("p u (r e) -> p u r e", e=PAIR)
+        def halves_of(t_bank):
+            return t_bank[:].bitcast(BF16).rearrange("p u (r e) -> p u r e", e=PAIR)
 
-        def mix_pass(g):
-            sx_t = transpose_pass(sx_sb, g, "sx_t")
-            x_t = transpose_pass(x_sb, g, "x_t")
-            kept = work.tile([P, PACK, ROWS], F32)
-            mixed = work.tile([P, PACK, ROWS], BF16)
+        BOTH = tuple(range(ROW_TILES))
+
+        sx_t_of = {}
+        x_t_of = {}
+        kept_of = {}
+        mixed_of = {}
+        grouped_of = {}
+
+        def turn_x(g):
+            sx_t_of[g] = transpose_pass(sx_sb, g, BOTH, 2 * g, "sx_t")
+            x_t_of[g] = transpose_pass(x_sb, g, BOTH, 2 * g + 1, "x_t")
+
+        def keep_part(g):
+            kept = work.tile([P, PACK, ROWS], F32, name="kept", bufs=GROUPS)
+            kept_of[g] = kept
             for t in range(PACK):
                 u, e = divmod(t, PAIR)
                 col = PACK * g + t
                 nc.scalar.activation(
                     out=kept[:, t, :],
-                    in_=halves_of(sx_t)[:, u, :, e],
+                    in_=halves_of(sx_t_of[g])[:, u, :, e],
                     func=ACT.Copy,
                     scale=one_minus_mix[:, col : col + 1],
                 )
+
+        def mix_part(g, ts):
+            if g not in mixed_of:
+                mixed_of[g] = work.tile([P, PACK, ROWS], BF16, name="mixed")
+            for t in ts:
+                u, e = divmod(t, PAIR)
+                col = PACK * g + t
                 nc.vector.scalar_tensor_tensor(
-                    out=mixed[:, t, :],
-                    in0=halves_of(x_t)[:, u, :, e],
+                    out=mixed_of[g][:, t, :],
+                    in0=halves_of(x_t_of[g])[:, u, :, e],
                     scalar=mix[:, col : col + 1],
-                    in1=kept[:, t, :],
+                    in1=kept_of[g][:, t, :],
                     op0=ALU.mult,
                     op1=ALU.add,
                 )
-            return mixed
 
         def group_planes(mixed):
             grouped = work.tile([P, ROWS, PACK], BF16, name="xr_grouped", align_bytes=64)
@@ -168,19 +197,19 @@ def tile_rwkv_timemix_for_quant_pb_kernel(
             )
             return grouped
 
-        def quantise(grouped, codes, scales, g):
+        def quantise(grouped, codes, scales, g, first, count):
             nc.vector.quantize_mx(
-                out=codes[:, g, :].bitcast(FP8X4),
-                scales=scales[:, g, :],
+                out=codes[:, g, first : first + count].bitcast(FP8X4),
+                scales=scales[:, g, first : first + count],
                 in_=grouped[:].rearrange("p r t -> p (r t)"),
             )
 
-        def accumulators(name):
-            return [psum.tile([P, N_TILE], F32, name="%s%d" % (name, r), tag="bank") for r in range(ROW_TILES)]
+        def accumulators(name, b0):
+            return [bank(b0 + r, [P, N_TILE], "%s%d" % (name, r)) for r in range(ROW_TILES)]
 
-        def product(acc, codes, scales, w_words, w_planes, c, g):
+        def product(acc, codes, scales, w_words, w_planes, c, g, rows=BOTH):
             first = c * N_TILE
-            for r in range(ROW_TILES):
+            for r in rows:
                 nc.tensor.matmul_mx(
                     out=acc[r][:],
                     lhsT=codes[:, g, r * P : (r + 1) * P].bitcast(FP8X4),
@@ -190,6 +219,12 @@ def tile_rwkv_timemix_for_quant_pb_kernel(
                     start=(g == 0),
                     stop=(g == GROUPS - 1),
                 )
+
+        def first_product(z, c, g):
+            product(z, xr_codes, xr_scales, wr_words, wr_planes, c, g)
+
+        def second_product(y, c, g, rows=BOTH):
+            product(y, h_codes, h_scales, wo_words, wo_planes, c, g, rows)
 
         def gate_root(c):
             cols = slice(c * N_TILE, (c + 1) * N_TILE)
@@ -205,24 +240,32 @@ def tile_rwkv_timemix_for_quant_pb_kernel(
             cols = slice(c * N_TILE, (c + 1) * N_TILE)
             nc.vector.tensor_mul(out=gate[:, :, cols], in0=num_sb[:, :, cols], in1=gate[:, :, cols])
 
-        def gated(z, c):
-            cols = slice(c * N_TILE, (c + 1) * N_TILE)
-            for r in range(ROW_TILES):
-                ramp = work.tile([P, N_TILE], F32, bufs=4)
+        ramp_of = {}
+
+        def ramp_up(z, c, rows=BOTH):
+            for r in rows:
+                ramp = work.tile([P, N_TILE], F32, name="ramp", bufs=RAMPS)
                 nc.scalar.activation(out=ramp[:], in_=z[r][:], func=ACT.Relu, bias=3.0)
+                ramp_of[(c, r)] = ramp
+
+        def gated(c, rows=BOTH):
+            cols = slice(c * N_TILE, (c + 1) * N_TILE)
+            for r in rows:
                 nc.vector.scalar_tensor_tensor(
                     out=h_sb[:, r, cols],
-                    in0=ramp[:],
+                    in0=ramp_of[(c, r)][:],
                     scalar=6.0,
                     in1=gate[:, r, cols],
                     op0=ALU.min,
                     op1=ALU.mult,
                 )
 
-        def group_h(g):
-            h_t = transpose_pass(h_sb, g, "h_t")
-            grouped = work.tile([P, ROWS, PACK], BF16, name="h_grouped", align_bytes=64)
-            nc.vector.tensor_copy(
+        def turn_h(g, rows, b):
+            return transpose_pass(h_sb, g, rows, b, "h_t")
+
+        def group_h(h_t, rows, engine_copy):
+            grouped = work.tile([P, len(rows) * P, PACK], BF16, name="h_grouped%d" % len(rows), align_bytes=64)
+            engine_copy(
                 out=grouped[:].rearrange("p r t -> p (r t)").bitcast(F32).rearrange("p (r u) -> p r u", u=PAIR),
                 in_=h_t[:].rearrange("p u r -> p r u"),
             )
@@ -237,57 +280,81 @@ def tile_rwkv_timemix_for_quant_pb_kernel(
             for r in range(ROW_TILES):
                 nc.sync.dma_start(out=out_rows[:, r, cols], in_=out_sb[:, r, cols])
 
-        mixed_of = {}
-        grouped_of = {}
-        for g in range(GROUPS + 2):
-            if g < GROUPS:
-                mixed_of[g] = mix_pass(g)
-            if 1 <= g <= GROUPS:
-                grouped_of[g - 1] = group_planes(mixed_of[g - 1])
-            if g >= 2:
-                quantise(grouped_of[g - 2], xr_codes, xr_scales, g - 2)
-
         z_of = {}
-        for c in range(EARLY):
-            z_of[c] = accumulators("z")
-        for g in range(GROUPS):
-            for c in range(EARLY):
-                product(z_of[c], xr_codes, xr_scales, wr_words, wr_planes, c, g)
-        gate_root(0)
-        gate_root(1)
-        gate_square(0)
-        gate_square(1)
-        gate_times_num(0)
-        for c in range(COL_TILES):
-            if c >= EARLY:
-                z_of[c] = accumulators("z")
-                for g in range(GROUPS):
-                    product(z_of[c], xr_codes, xr_scales, wr_words, wr_planes, c, g)
-            if c >= 1:
-                h_grouped = group_h(c - 1)
-            if c + 2 < COL_TILES:
-                gate_root(c + 2)
-            gated(z_of[c], c)
-            if c >= 1:
-                quantise(h_grouped, h_codes, h_scales, c - 1)
-            if c + 1 < COL_TILES:
-                gate_times_num(c + 1)
-            if c + 2 < COL_TILES:
-                gate_square(c + 2)
-
         y_of = {}
-        for c in range(EARLY):
-            y_of[c] = accumulators("y")
+        hq = {}
+        ht = {}
         for g in range(GROUPS):
-            if g == GROUPS - 2:
-                h_grouped = group_h(COL_TILES - 1)
-                quantise(h_grouped, h_codes, h_scales, COL_TILES - 1)
+            turn_x(g)
+            keep_part(g)
+        gate_root(0)
+        gate_square(0)
+        gate_root(1)
+        gate_square(1)
+        gate_root(2)
+        mix_part(0, range(PACK))
+        for g in range(GROUPS):
+            if g + 1 < GROUPS:
+                mix_part(g + 1, (0, 1))
+            grouped_of[g] = group_planes(mixed_of[g])
+            if g + 1 < GROUPS:
+                mix_part(g + 1, (2, 3))
+            quantise(grouped_of[g], xr_codes, xr_scales, g, 0, ROWS)
             for c in range(EARLY):
-                product(y_of[c], h_codes, h_scales, wo_words, wo_planes, c, g)
-        for c in range(EARLY):
+                if g == 0:
+                    z_of[c] = accumulators("z", 2 * c)
+                first_product(z_of[c], c, g)
+        gate_times_num(0)
+        ramp_up(z_of[0], 0)
+        gated(0)
+        ramp_up(z_of[1], 1)
+        gate_times_num(1)
+        gated(1)
+        z_of[2] = accumulators("z", 4)
+        for g in range(GROUPS):
+            first_product(z_of[2], 2, g)
+        ht[0] = turn_h(0, BOTH, 0)
+        gate_square(2)
+        hq[0] = group_h(ht[0], BOTH, nc.scalar.copy)
+        gate_times_num(2)
+        quantise(hq[0], h_codes, h_scales, 0, 0, ROWS)
+        z_of[3] = accumulators("z", 6)
+        for g in range(GROUPS):
+            first_product(z_of[3], 3, g)
+        gate_root(3)
+        ramp_up(z_of[2], 2)
+        gated(2)
+        ht[1] = turn_h(1, BOTH, 1)
+        hq[1] = group_h(ht[1], BOTH, nc.vector.tensor_copy)
+        gate_square(3)
+        ramp_up(z_of[3], 3)
+        quantise(hq[1], h_codes, h_scales, 1, 0, ROWS)
+        gate_times_num(3)
+        y_of[0] = accumulators("y", 2)
+        y_of[1] = accumulators("y", 4)
+        for c in range(2):
+            second_product(y_of[c], c, 0)
+        ht[2] = turn_h(2, BOTH, 0)
+        y_of[2] = accumulators("y", 6)
+        second_product(y_of[2], 2, 0)
+        for c in range(LATE):
+            second_product(y_of[c], c, 1)
+        gated(3, (0,))
+        hq[2] = group_h(ht[2], BOTH, nc.scalar.copy)
+        ht[3] = turn_h(3, (0,), 1)
+        gated(3, (1,))
+        quantise(hq[2], h_codes, h_scales, 2, 0, ROWS)
+        hq[3] = group_h(ht[3], (0,), nc.scalar.copy)
+        quantise(hq[3], h_codes, h_scales, 3, 0, P)
+        ht[4] = turn_h(3, (1,), 0)
+        hq[4] = group_h(ht[4], (1,), nc.scalar.copy)
+        quantise(hq[4], h_codes, h_scales, 3, P, P)
+        for c in range(LATE):
+            second_product(y_of[c], c, 2)
+        for c in range(LATE):
+            second_product(y_of[c], c, 3)
             leave(y_of[c], c)
-        for c in range(EARLY, COL_TILES):
-            y_of[c] = accumulators("y")
-            for g in range(GROUPS):
-                product(y_of[c], h_codes, h_scales, wo_words, wo_planes, c, g)
-            leave(y_of[c], c)
+        y_of[3] = accumulators("y", 0)
+        for g in range(GROUPS):
+            second_product(y_of[3], 3, g)
+        leave(y_of[3], 3)

@@ -66,7 +66,7 @@ def tile_rwkv_timemix_for_quant_pb_kernel(
         h_codes = keep.tile([P, GROUPS, ROWS], U32, align_bytes=64)
         h_scales = keep.tile([P, GROUPS, ROWS], U8, align_bytes=64)
         ident = keep.tile([P, P], F32)
-        mix_bf = keep.tile([P, GROUPS, PACK], BF16)
+        mix_rows = keep.tile([P, K_PASS], BF16)
         mix = keep.tile([P, GROUPS * PACK], F32)
         one_minus_mix = keep.tile([P, GROUPS * PACK], F32)
         warm = keep.tile([P, 1], F32)
@@ -74,19 +74,27 @@ def tile_rwkv_timemix_for_quant_pb_kernel(
         def bank(b, shape, name):
             return psum.tile(shape, F32, name=name, tag="bank%d" % b)
 
+        nc.gpsimd.memset(mix_rows[:], 0.0)
         nc.scalar.dma_start(
-            out=mix_bf[:],
-            in_=time_mix_r.rearrange("o (g p t) -> p (o g) t", g=GROUPS, p=P, t=PACK),
+            out=mix_rows[0:GROUPS, :], in_=time_mix_r.rearrange("o (g k) -> (o g) k", g=GROUPS)
         )
         nc.vector.memset(wr_planes[:].bitcast(I32), 0)
         nc.vector.memset(wo_planes[:].bitcast(I32), 0)
         nc.vector.memset(warm[:], 1.0)
         nc.scalar.activation(out=warm[:], in_=warm[:], func=ACT.Abs_reciprocal_sqrt)
         make_identity(nc, ident[:])
-        mix_flat = mix_bf[:].rearrange("p g t -> p (g t)")
-        nc.vector.tensor_copy(out=mix[:], in_=mix_flat)
+        mix_t = bank(7, [P, PAIR, P], "mix_t")
+        for u in range(PAIR):
+            nc.tensor.transpose(mix_t[:, u, :], mix_rows[:].bitcast(F32)[:, u::PAIR], ident[:])
+        mix_pairs = mix_t[:].bitcast(BF16).rearrange("p u (r e) -> p r u e", e=PAIR)[:, 0:GROUPS]
+        nc.vector.tensor_copy(out=mix[:].rearrange("p (g u e) -> p g u e", u=PAIR, e=PAIR), in_=mix_pairs)
         nc.vector.tensor_scalar(
-            out=one_minus_mix[:], in0=mix_flat, scalar1=-1.0, scalar2=1.0, op0=ALU.mult, op1=ALU.add
+            out=one_minus_mix[:].rearrange("p (g u e) -> p g u e", u=PAIR, e=PAIR),
+            in0=mix_pairs,
+            scalar1=-1.0,
+            scalar2=1.0,
+            op0=ALU.mult,
+            op1=ALU.add,
         )
 
         def load_rows(dst, src, first, count):
@@ -123,12 +131,14 @@ def tile_rwkv_timemix_for_quant_pb_kernel(
         load_rows(den_sb, wkv_den, 0, HALF)
         load_words(wr_words, W_receptance_words, 0, EARLY, (1,))
         load_rows(den_sb, wkv_den, HALF, HALF)
-        load_planes(wo_planes, W_output_scales)
-        load_words(wr_words, W_receptance_words, 0, EARLY, (2, 3))
-        load_rows(num_sb, wkv_num, 0, HALF)
+        load_words(wr_words, W_receptance_words, 0, EARLY, (2,))
+        load_rows(num_sb, wkv_num, 0, N_TILE)
+        load_words(wr_words, W_receptance_words, 0, EARLY, (3,))
+        load_rows(num_sb, wkv_num, N_TILE, N_TILE)
         load_words(wr_words, W_receptance_words, 2, 1, range(GROUPS))
         load_rows(num_sb, wkv_num, HALF, HALF)
         load_words(wr_words, W_receptance_words, 3, 1, range(GROUPS))
+        load_planes(wo_planes, W_output_scales)
         for c in range(LATE):
             load_words(wo_words, W_output_words, c, 1, (0,))
         load_words(wo_words, W_output_words, 0, LATE, range(1, GROUPS))
@@ -189,11 +199,11 @@ def tile_rwkv_timemix_for_quant_pb_kernel(
                     op1=ALU.add,
                 )
 
-        def group_planes(mixed):
-            grouped = work.tile([P, ROWS, PACK], BF16, name="xr_grouped", align_bytes=64)
+        def group_planes(mixed, first, count):
+            grouped = work.tile([P, count, PACK], BF16, name="xr_grouped%d" % count, align_bytes=64)
             nc.vector.tensor_copy(
                 out=grouped[:].rearrange("p (c i) t -> p c t i", i=4),
-                in_=mixed[:].rearrange("p t (c i) -> p c t i", i=4),
+                in_=mixed[:, :, first : first + count].rearrange("p t (c i) -> p c t i", i=4),
             )
             return grouped
 
@@ -288,27 +298,32 @@ def tile_rwkv_timemix_for_quant_pb_kernel(
             turn_x(g)
             keep_part(g)
         gate_root(0)
-        gate_square(0)
         gate_root(1)
+        gate_square(0)
         gate_square(1)
         gate_root(2)
         mix_part(0, range(PACK))
-        for g in range(GROUPS):
-            if g + 1 < GROUPS:
-                mix_part(g + 1, (0, 1))
-            grouped_of[g] = group_planes(mixed_of[g])
-            if g + 1 < GROUPS:
-                mix_part(g + 1, (2, 3))
+        for g in range(GROUPS - 1):
+            mix_part(g + 1, (0, 1))
+            grouped_of[g] = group_planes(mixed_of[g], 0, ROWS)
+            mix_part(g + 1, (2, 3))
             quantise(grouped_of[g], xr_codes, xr_scales, g, 0, ROWS)
             for c in range(EARLY):
                 if g == 0:
                     z_of[c] = accumulators("z", 2 * c)
                 first_product(z_of[c], c, g)
+        last = GROUPS - 1
+        for r in range(ROW_TILES):
+            grouped_of[(last, r)] = group_planes(mixed_of[last], r * P, P)
+        for r in range(ROW_TILES):
+            quantise(grouped_of[(last, r)], xr_codes, xr_scales, last, r * P, P)
+        for c in range(EARLY):
+            first_product(z_of[c], c, last)
         gate_times_num(0)
+        gate_times_num(1)
         ramp_up(z_of[0], 0)
         gated(0)
         ramp_up(z_of[1], 1)
-        gate_times_num(1)
         gated(1)
         z_of[2] = accumulators("z", 4)
         for g in range(GROUPS):
@@ -323,9 +338,9 @@ def tile_rwkv_timemix_for_quant_pb_kernel(
             first_product(z_of[3], 3, g)
         gate_root(3)
         ramp_up(z_of[2], 2)
-        gated(2)
         ht[1] = turn_h(1, BOTH, 1)
         hq[1] = group_h(ht[1], BOTH, nc.vector.tensor_copy)
+        gated(2)
         gate_square(3)
         ramp_up(z_of[3], 3)
         quantise(hq[1], h_codes, h_scales, 1, 0, ROWS)
@@ -339,11 +354,11 @@ def tile_rwkv_timemix_for_quant_pb_kernel(
         second_product(y_of[2], 2, 0)
         for c in range(LATE):
             second_product(y_of[c], c, 1)
-        gated(3, (0,))
         hq[2] = group_h(ht[2], BOTH, nc.scalar.copy)
+        quantise(hq[2], h_codes, h_scales, 2, 0, ROWS)
+        gated(3, (0,))
         ht[3] = turn_h(3, (0,), 1)
         gated(3, (1,))
-        quantise(hq[2], h_codes, h_scales, 2, 0, ROWS)
         hq[3] = group_h(ht[3], (0,), nc.scalar.copy)
         quantise(hq[3], h_codes, h_scales, 3, 0, P)
         ht[4] = turn_h(3, (1,), 0)

@@ -75,32 +75,20 @@ def tile_rwkv_timemix_for_quant_pb_kernel(
             return psum.tile(shape, F32, name=name, tag="bank%d" % b)
 
         nc.gpsimd.memset(mix_rows[:], 0.0)
-        nc.scalar.dma_start(
-            out=mix_rows[0:GROUPS, :], in_=time_mix_r.rearrange("o (g k) -> (o g) k", g=GROUPS)
-        )
         nc.vector.memset(wr_planes[:].bitcast(I32), 0)
         nc.vector.memset(wo_planes[:].bitcast(I32), 0)
         nc.vector.memset(warm[:], 1.0)
         nc.scalar.activation(out=warm[:], in_=warm[:], func=ACT.Abs_reciprocal_sqrt)
         make_identity(nc, ident[:])
-        mix_t = bank(7, [P, PAIR, P], "mix_t")
-        for u in range(PAIR):
-            nc.tensor.transpose(mix_t[:, u, :], mix_rows[:].bitcast(F32)[:, u::PAIR], ident[:])
-        mix_pairs = mix_t[:].bitcast(BF16).rearrange("p u (r e) -> p r u e", e=PAIR)[:, 0:GROUPS]
-        nc.vector.tensor_copy(out=mix[:].rearrange("p (g u e) -> p g u e", u=PAIR, e=PAIR), in_=mix_pairs)
-        nc.vector.tensor_scalar(
-            out=one_minus_mix[:].rearrange("p (g u e) -> p g u e", u=PAIR, e=PAIR),
-            in0=mix_pairs,
-            scalar1=-1.0,
-            scalar2=1.0,
-            op0=ALU.mult,
-            op1=ALU.add,
-        )
-
         def load_rows(dst, src, first, count):
             nc.sync.dma_start(
                 out=dst[:, :, first : first + count],
                 in_=src.rearrange("(r p) e -> p r e", p=P)[:, :, first : first + count],
+            )
+
+        def load_mix():
+            nc.sync.dma_start(
+                out=mix_rows[0:GROUPS, :], in_=time_mix_r.rearrange("o (g k) -> (o g) k", g=GROUPS)
             )
 
         def load_planes(planes, scales):
@@ -121,16 +109,16 @@ def tile_rwkv_timemix_for_quant_pb_kernel(
                 )
 
         HALF = WIDTH // 2
-        for g in range(2):
-            load_rows(sx_sb, state_x, g * K_PASS, K_PASS)
-            load_rows(x_sb, x, g * K_PASS, K_PASS)
-        load_rows(sx_sb, state_x, HALF, HALF)
-        load_rows(x_sb, x, HALF, HALF)
+        REST = WIDTH - K_PASS
+        load_rows(sx_sb, state_x, 0, K_PASS)
+        load_rows(x_sb, x, 0, K_PASS)
+        load_mix()
+        load_rows(sx_sb, state_x, K_PASS, REST)
+        load_rows(x_sb, x, K_PASS, REST)
         load_planes(wr_planes, W_receptance_scales)
         load_words(wr_words, W_receptance_words, 0, EARLY, (0,))
-        load_rows(den_sb, wkv_den, 0, HALF)
+        load_rows(den_sb, wkv_den, 0, WIDTH)
         load_words(wr_words, W_receptance_words, 0, EARLY, (1,))
-        load_rows(den_sb, wkv_den, HALF, HALF)
         load_words(wr_words, W_receptance_words, 0, EARLY, (2,))
         load_rows(num_sb, wkv_num, 0, N_TILE)
         load_words(wr_words, W_receptance_words, 0, EARLY, (3,))
@@ -143,6 +131,20 @@ def tile_rwkv_timemix_for_quant_pb_kernel(
             load_words(wo_words, W_output_words, c, 1, (0,))
         load_words(wo_words, W_output_words, 0, LATE, range(1, GROUPS))
         load_words(wo_words, W_output_words, LATE, 1, range(GROUPS))
+
+        mix_t = bank(7, [P, PAIR, P], "mix_t")
+        for u in range(PAIR):
+            nc.tensor.transpose(mix_t[:, u, :], mix_rows[:].bitcast(F32)[:, u::PAIR], ident[:])
+        mix_pairs = mix_t[:].bitcast(BF16).rearrange("p u (r e) -> p r u e", e=PAIR)[:, 0:GROUPS]
+        nc.vector.tensor_copy(out=mix[:].rearrange("p (g u e) -> p g u e", u=PAIR, e=PAIR), in_=mix_pairs)
+        nc.vector.tensor_scalar(
+            out=one_minus_mix[:].rearrange("p (g u e) -> p g u e", u=PAIR, e=PAIR),
+            in0=mix_pairs,
+            scalar1=-1.0,
+            scalar2=1.0,
+            op0=ALU.mult,
+            op1=ALU.add,
+        )
 
         def transpose_pass(src, g, rows, b, name):
             t_bank = bank(b, [P, PAIR, len(rows) * P], name)
@@ -217,15 +219,16 @@ def tile_rwkv_timemix_for_quant_pb_kernel(
         def accumulators(name, b0):
             return [bank(b0 + r, [P, N_TILE], "%s%d" % (name, r)) for r in range(ROW_TILES)]
 
-        def product(acc, codes, scales, w_words, w_planes, c, g, rows=BOTH):
-            first = c * N_TILE
+        def product(acc, codes, scales, w_words, w_planes, c, g, rows=BOTH, first=None, count=N_TILE):
+            if first is None:
+                first = c * N_TILE
             for r in rows:
                 nc.tensor.matmul_mx(
-                    out=acc[r][:],
+                    out=acc[r][:, 0:count],
                     lhsT=codes[:, g, r * P : (r + 1) * P].bitcast(FP8X4),
                     lhsT_scale=scales[:, g, r * P : (r + 1) * P],
-                    rhs=w_words[:, g, first : first + N_TILE].bitcast(FP8X4),
-                    rhs_scale=w_planes[PACK * g : P, first : first + N_TILE],
+                    rhs=w_words[:, g, first : first + count].bitcast(FP8X4),
+                    rhs_scale=w_planes[PACK * g : P, first : first + count],
                     start=(g == 0),
                     stop=(g == GROUPS - 1),
                 )
@@ -233,8 +236,8 @@ def tile_rwkv_timemix_for_quant_pb_kernel(
         def first_product(z, c, g):
             product(z, xr_codes, xr_scales, wr_words, wr_planes, c, g)
 
-        def second_product(y, c, g, rows=BOTH):
-            product(y, h_codes, h_scales, wo_words, wo_planes, c, g, rows)
+        def second_product(y, c, g, rows=BOTH, first=None, count=N_TILE):
+            product(y, h_codes, h_scales, wo_words, wo_planes, c, g, rows, first, count)
 
         def gate_root(c):
             cols = slice(c * N_TILE, (c + 1) * N_TILE)
@@ -283,10 +286,12 @@ def tile_rwkv_timemix_for_quant_pb_kernel(
 
         out_rows = out.rearrange("(r p) e -> p r e", p=P)
 
-        def leave(y, c):
-            cols = slice(c * N_TILE, (c + 1) * N_TILE)
-            nc.scalar.copy(out=out_sb[:, 0, cols], in_=y[0][:])
-            nc.vector.tensor_copy(out=out_sb[:, 1, cols], in_=y[1][:])
+        def leave(y, c, first=None, count=N_TILE):
+            if first is None:
+                first = c * N_TILE
+            cols = slice(first, first + count)
+            nc.scalar.copy(out=out_sb[:, 0, cols], in_=y[0][:, 0:count])
+            nc.vector.tensor_copy(out=out_sb[:, 1, cols], in_=y[1][:, 0:count])
             for r in range(ROW_TILES):
                 nc.sync.dma_start(out=out_rows[:, r, cols], in_=out_sb[:, r, cols])
 
@@ -366,10 +371,11 @@ def tile_rwkv_timemix_for_quant_pb_kernel(
         quantise(hq[4], h_codes, h_scales, 3, P, P)
         for c in range(LATE):
             second_product(y_of[c], c, 2)
-        for c in range(LATE):
             second_product(y_of[c], c, 3)
             leave(y_of[c], c)
-        y_of[3] = accumulators("y", 0)
-        for g in range(GROUPS):
-            second_product(y_of[3], 3, g)
-        leave(y_of[3], 3)
+        for half in range(2):
+            y_last = accumulators("y", 2 * half)
+            first = LATE * N_TILE + half * (N_TILE // 2)
+            for g in range(GROUPS):
+                second_product(y_last, LATE, g, BOTH, first, N_TILE // 2)
+            leave(y_last, LATE, first, N_TILE // 2)

@@ -115,21 +115,21 @@ def tile_rwkv_timemix_for_quant_pb_kernel(
         load_mix()
         load_rows(sx_sb, state_x, K_PASS, REST)
         load_rows(x_sb, x, K_PASS, REST)
-        load_planes(wr_planes, W_receptance_scales)
-        load_words(wr_words, W_receptance_words, 0, EARLY, (0,))
         load_rows(den_sb, wkv_den, 0, WIDTH)
-        load_words(wr_words, W_receptance_words, 0, EARLY, (1,))
-        load_words(wr_words, W_receptance_words, 0, EARLY, (2,))
-        load_rows(num_sb, wkv_num, 0, N_TILE)
+        load_planes(wr_planes, W_receptance_scales)
+        load_words(wr_words, W_receptance_words, 0, EARLY, (0, 1, 2))
+        load_rows(num_sb, wkv_num, 0, HALF)
         load_words(wr_words, W_receptance_words, 0, EARLY, (3,))
-        load_rows(num_sb, wkv_num, N_TILE, N_TILE)
         load_words(wr_words, W_receptance_words, 2, 1, range(GROUPS))
         load_rows(num_sb, wkv_num, HALF, HALF)
         load_words(wr_words, W_receptance_words, 3, 1, range(GROUPS))
         load_planes(wo_planes, W_output_scales)
+        for g in range(2):
+            for c in range(LATE):
+                load_words(wo_words, W_output_words, c, 1, (g,))
+        load_words(wo_words, W_output_words, 0, LATE, (2,))
         for c in range(LATE):
-            load_words(wo_words, W_output_words, c, 1, (0,))
-        load_words(wo_words, W_output_words, 0, LATE, range(1, GROUPS))
+            load_words(wo_words, W_output_words, c, 1, (GROUPS - 1,))
         load_words(wo_words, W_output_words, LATE, 1, range(GROUPS))
 
         mix_t = bank(7, [P, PAIR, P], "mix_t")
@@ -307,6 +307,7 @@ def tile_rwkv_timemix_for_quant_pb_kernel(
         gate_square(0)
         gate_square(1)
         gate_root(2)
+        gate_root(3)
         mix_part(0, range(PACK))
         for g in range(GROUPS - 1):
             mix_part(g + 1, (0, 1))
@@ -334,41 +335,41 @@ def tile_rwkv_timemix_for_quant_pb_kernel(
         for g in range(GROUPS):
             first_product(z_of[2], 2, g)
         ht[0] = turn_h(0, BOTH, 0)
+        ht[1] = turn_h(1, BOTH, 1)
         gate_square(2)
-        hq[0] = group_h(ht[0], BOTH, nc.scalar.copy)
+        ramp_up(z_of[2], 2)
         gate_times_num(2)
+        gated(2)
+        hq[0] = group_h(ht[0], BOTH, nc.scalar.copy)
+        hq[1] = group_h(ht[1], BOTH, nc.scalar.copy)
         quantise(hq[0], h_codes, h_scales, 0, 0, ROWS)
+        quantise(hq[1], h_codes, h_scales, 1, 0, ROWS)
         z_of[3] = accumulators("z", 6)
         for g in range(GROUPS):
             first_product(z_of[3], 3, g)
-        gate_root(3)
-        ramp_up(z_of[2], 2)
-        ht[1] = turn_h(1, BOTH, 1)
-        hq[1] = group_h(ht[1], BOTH, nc.vector.tensor_copy)
-        gated(2)
         gate_square(3)
-        ramp_up(z_of[3], 3)
-        quantise(hq[1], h_codes, h_scales, 1, 0, ROWS)
         gate_times_num(3)
+        ht[2] = turn_h(2, BOTH, 0)
+        ramp_up(z_of[3], 3)
         y_of[0] = accumulators("y", 2)
         y_of[1] = accumulators("y", 4)
         for c in range(2):
             second_product(y_of[c], c, 0)
-        ht[2] = turn_h(2, BOTH, 0)
         y_of[2] = accumulators("y", 6)
         second_product(y_of[2], 2, 0)
-        for c in range(LATE):
-            second_product(y_of[c], c, 1)
+        gated(3, (0,))
+        gated(3, (1,))
         hq[2] = group_h(ht[2], BOTH, nc.scalar.copy)
         quantise(hq[2], h_codes, h_scales, 2, 0, ROWS)
-        gated(3, (0,))
+        for c in range(EARLY):
+            second_product(y_of[c], c, 1)
         ht[3] = turn_h(3, (0,), 1)
-        gated(3, (1,))
-        hq[3] = group_h(ht[3], (0,), nc.scalar.copy)
-        quantise(hq[3], h_codes, h_scales, 3, 0, P)
         ht[4] = turn_h(3, (1,), 0)
+        hq[3] = group_h(ht[3], (0,), nc.scalar.copy)
         hq[4] = group_h(ht[4], (1,), nc.scalar.copy)
+        quantise(hq[3], h_codes, h_scales, 3, 0, P)
         quantise(hq[4], h_codes, h_scales, 3, P, P)
+        second_product(y_of[2], 2, 1)
         for c in range(LATE):
             second_product(y_of[c], c, 2)
             second_product(y_of[c], c, 3)

@@ -57,14 +57,14 @@ def tile_rwkv_timemix_for_quant_pb_kernel(
         h_sb = keep.tile([P, ROW_TILES, WIDTH], BF16)
         gate = keep.tile([P, ROW_TILES, WIDTH], F32)
         out_sb = keep.tile([P, ROW_TILES, WIDTH], F32)
-        wr_words = keep.tile([P, GROUPS, WIDTH], U32, align_bytes=64)
-        wo_words = keep.tile([P, GROUPS, WIDTH], U32, align_bytes=64)
-        wr_planes = keep.tile([P, WIDTH], U8, align_bytes=64)
-        wo_planes = keep.tile([P, WIDTH], U8, align_bytes=64)
-        xr_codes = keep.tile([P, GROUPS, ROWS], U32, align_bytes=64)
-        xr_scales = keep.tile([P, GROUPS, ROWS], U8, align_bytes=64)
-        h_codes = keep.tile([P, GROUPS, ROWS], U32, align_bytes=64)
-        h_scales = keep.tile([P, GROUPS, ROWS], U8, align_bytes=64)
+        wr_words = keep.tile([P, GROUPS, WIDTH], U32, align_bytes=256)
+        wo_words = keep.tile([P, GROUPS, WIDTH], U32, align_bytes=256)
+        wr_planes = keep.tile([P, WIDTH], U8, align_bytes=256)
+        wo_planes = keep.tile([P, WIDTH], U8, align_bytes=256)
+        xr_codes = keep.tile([P, GROUPS, ROWS], U32, align_bytes=256)
+        xr_scales = keep.tile([P, GROUPS, ROWS], U8, align_bytes=256)
+        h_codes = keep.tile([P, GROUPS, ROWS], U32, align_bytes=256)
+        h_scales = keep.tile([P, GROUPS, ROWS], U8, align_bytes=256)
         ident = keep.tile([P, P], F32)
         mix_rows = keep.tile([P, K_PASS], BF16)
         mix = keep.tile([P, GROUPS * PACK], F32)
@@ -202,7 +202,7 @@ def tile_rwkv_timemix_for_quant_pb_kernel(
                 )
 
         def group_planes(mixed, first, count):
-            grouped = work.tile([P, count, PACK], BF16, name="xr_grouped%d" % count, align_bytes=64)
+            grouped = work.tile([P, count, PACK], BF16, name="xr_grouped%d" % count, align_bytes=256)
             nc.vector.tensor_copy(
                 out=grouped[:].rearrange("p (c i) t -> p c t i", i=4),
                 in_=mixed[:, :, first : first + count].rearrange("p t (c i) -> p c t i", i=4),
@@ -277,7 +277,7 @@ def tile_rwkv_timemix_for_quant_pb_kernel(
             return transpose_pass(h_sb, g, rows, b, "h_t")
 
         def group_h(h_t, rows, engine_copy):
-            grouped = work.tile([P, len(rows) * P, PACK], BF16, name="h_grouped%d" % len(rows), align_bytes=64)
+            grouped = work.tile([P, len(rows) * P, PACK], BF16, name="h_grouped%d" % len(rows), align_bytes=256)
             engine_copy(
                 out=grouped[:].rearrange("p r t -> p (r t)").bitcast(F32).rearrange("p (r u) -> p r u", u=PAIR),
                 in_=h_t[:].rearrange("p u r -> p r u"),

@@ -50,13 +50,13 @@ def tile_rwkv_timemix_for_quant_pb_kernel(
         psum = ctx.enter_context(tc.psum_pool(name="psum", bufs=1))
         ctx.enter_context(tc.manual_schedule())
 
-        x_sb = keep.tile([P, ROW_TILES, WIDTH], BF16)
-        sx_sb = keep.tile([P, ROW_TILES, WIDTH], BF16)
-        num_sb = keep.tile([P, ROW_TILES, WIDTH], BF16)
-        den_sb = keep.tile([P, ROW_TILES, WIDTH], BF16)
-        h_sb = keep.tile([P, ROW_TILES, WIDTH], BF16)
-        gate = keep.tile([P, ROW_TILES, WIDTH], F32)
-        out_sb = keep.tile([P, ROW_TILES, WIDTH], F32)
+        x_sb = keep.tile([P, ROW_TILES, WIDTH], BF16, align_bytes=256)
+        sx_sb = keep.tile([P, ROW_TILES, WIDTH], BF16, align_bytes=256)
+        num_sb = keep.tile([P, ROW_TILES, WIDTH], BF16, align_bytes=256)
+        den_sb = keep.tile([P, ROW_TILES, WIDTH], BF16, align_bytes=256)
+        h_sb = keep.tile([P, ROW_TILES, WIDTH], BF16, align_bytes=256)
+        gate = keep.tile([P, ROW_TILES, WIDTH], F32, align_bytes=256)
+        out_sb = keep.tile([P, ROW_TILES, WIDTH], F32, align_bytes=256)
         wr_words = keep.tile([P, GROUPS, WIDTH], U32, align_bytes=256)
         wo_words = keep.tile([P, GROUPS, WIDTH], U32, align_bytes=256)
         wr_planes = keep.tile([P, WIDTH], U8, align_bytes=256)
@@ -65,8 +65,8 @@ def tile_rwkv_timemix_for_quant_pb_kernel(
         xr_scales = keep.tile([P, GROUPS, ROWS], U8, align_bytes=256)
         h_codes = keep.tile([P, GROUPS, ROWS], U32, align_bytes=256)
         h_scales = keep.tile([P, GROUPS, ROWS], U8, align_bytes=256)
-        ident = keep.tile([P, P], F32)
-        mix_rows = keep.tile([P, K_PASS], BF16)
+        ident = keep.tile([P, P], F32, align_bytes=256)
+        mix_rows = keep.tile([P, K_PASS], BF16, align_bytes=256)
         mix = keep.tile([P, GROUPS * PACK], F32)
         one_minus_mix = keep.tile([P, GROUPS * PACK], F32)
         warm = keep.tile([P, 1], F32)

@@ -174,7 +174,7 @@ def tile_rwkv_timemix_for_quant_pb_kernel(
             x_t_of[g] = transpose_pass(x_sb, g, BOTH, 2 * g + 1, "x_t")
 
         def keep_part(g):
-            kept = work.tile([P, PACK, ROWS], F32, name="kept", bufs=GROUPS)
+            kept = work.tile([P, PACK, ROWS], F32, name="kept", bufs=GROUPS, align_bytes=256)
             kept_of[g] = kept
             for t in range(PACK):
                 u, e = divmod(t, PAIR)
@@ -188,7 +188,7 @@ def tile_rwkv_timemix_for_quant_pb_kernel(
 
         def mix_part(g, ts):
             if g not in mixed_of:
-                mixed_of[g] = work.tile([P, PACK, ROWS], BF16, name="mixed")
+                mixed_of[g] = work.tile([P, PACK, ROWS], BF16, name="mixed", align_bytes=256)
             for t in ts:
                 u, e = divmod(t, PAIR)
                 col = PACK * g + t
@@ -257,7 +257,7 @@ def tile_rwkv_timemix_for_quant_pb_kernel(
 
         def ramp_up(z, c, rows=BOTH):
             for r in rows:
-                ramp = work.tile([P, N_TILE], F32, name="ramp", bufs=RAMPS)
+                ramp = work.tile([P, N_TILE], F32, name="ramp", bufs=RAMPS, align_bytes=256)
                 nc.scalar.activation(out=ramp[:], in_=z[r][:], func=ACT.Relu, bias=3.0)
                 ramp_of[(c, r)] = ramp
 

from contextlib import ExitStack

import concourse.mybir as mybir
from concourse.masks import make_identity

F32 = mybir.dt.float32
BF16 = mybir.dt.bfloat16
I32 = mybir.dt.int32
U32 = mybir.dt.uint32
U8 = mybir.dt.uint8
FP8X4 = mybir.dt.float8_e4m3fn_x4
ACT = mybir.ActivationFunctionType
ALU = mybir.AluOpType

P = 128
ROWS = 256
ROW_TILES = ROWS // P
WIDTH = 2048
PACK = 4
K_PASS = P * PACK
GROUPS = WIDTH // K_PASS
N_TILE = 512
COL_TILES = WIDTH // N_TILE
EARLY = 2
PAIR = 2
WORDS_PASS = K_PASS // PAIR

RAMPS = 4
LATE = 3
FLOPS = 2 * 2 * ROWS * WIDTH * WIDTH


def tile_rwkv_timemix_for_quant_pb_kernel(
    tc,
    x,
    state_x,
    time_mix_r,
    W_receptance_words,
    W_receptance_scales,
    wkv_num,
    wkv_den,
    W_output_words,
    W_output_scales,
    out,
):
    nc = tc.nc
    with ExitStack() as ctx:
        keep = ctx.enter_context(tc.tile_pool(name="keep", bufs=1))
        work = ctx.enter_context(tc.tile_pool(name="work", bufs=2))
        psum = ctx.enter_context(tc.psum_pool(name="psum", bufs=1))
        ctx.enter_context(tc.manual_schedule())

        x_sb = keep.tile([P, ROW_TILES, WIDTH], BF16, align_bytes=256)
        sx_sb = keep.tile([P, ROW_TILES, WIDTH], BF16, align_bytes=256)
        num_sb = keep.tile([P, ROW_TILES, WIDTH], BF16, align_bytes=256)
        den_sb = keep.tile([P, ROW_TILES, WIDTH], BF16, align_bytes=256)
        h_sb = keep.tile([P, ROW_TILES, WIDTH], BF16, align_bytes=256)
        gate = keep.tile([P, ROW_TILES, WIDTH], F32, align_bytes=256)
        out_sb = keep.tile([P, ROW_TILES, WIDTH], F32, align_bytes=256)
        wr_words = keep.tile([P, GROUPS, WIDTH], U32, align_bytes=256)
        wo_words = keep.tile([P, GROUPS, WIDTH], U32, align_bytes=256)
        wr_planes = keep.tile([P, WIDTH], U8, align_bytes=256)
        wo_planes = keep.tile([P, WIDTH], U8, align_bytes=256)
        xr_codes = keep.tile([P, GROUPS, ROWS], U32, align_bytes=256)
        xr_scales = keep.tile([P, GROUPS, ROWS], U8, align_bytes=256)
        h_codes = keep.tile([P, GROUPS, ROWS], U32, align_bytes=256)
        h_scales = keep.tile([P, GROUPS, ROWS], U8, align_bytes=256)
        ident = keep.tile([P, P], F32, align_bytes=256)
        mix_rows = keep.tile([P, K_PASS], BF16, align_bytes=256)
        mix = keep.tile([P, GROUPS * PACK], F32)
        one_minus_mix = keep.tile([P, GROUPS * PACK], F32)
        warm = keep.tile([P, 1], F32)

        def bank(b, shape, name):
            return psum.tile(shape, F32, name=name, tag="bank%d" % b)

        nc.gpsimd.memset(mix_rows[:], 0.0)
        nc.vector.memset(wr_planes[:].bitcast(I32), 0)
        nc.vector.memset(wo_planes[:].bitcast(I32), 0)
        nc.vector.memset(warm[:], 1.0)
        nc.scalar.activation(out=warm[:], in_=warm[:], func=ACT.Abs_reciprocal_sqrt)
        make_identity(nc, ident[:])
        def load_rows(dst, src, first, count):
            nc.sync.dma_start(
                out=dst[:, :, first : first + count],
                in_=src.rearrange("(r p) e -> p r e", p=P)[:, :, first : first + count],
            )

        def load_mix():
            nc.sync.dma_start(
                out=mix_rows[0:GROUPS, :], in_=time_mix_r.rearrange("o (g k) -> (o g) k", g=GROUPS)
            )

        def load_planes(planes, scales):
            for quad in range(4):
                nc.sync.dma_start(
                    out=planes[32 * quad : 32 * quad + 16, :].bitcast(I32),
                    in_=scales[:, 4 * quad : 4 * quad + 4, :].bitcast(I32),
                )

        def load_words(dst, words, first_tile, tiles, groups):
            first = first_tile * N_TILE
            count = tiles * N_TILE
            for g in groups:
                packed = words[g].rearrange("p n t -> p (n t)")
                nc.sync.dma_start(
                    out=dst[:, g, first : first + count].bitcast(I32),
                    in_=packed[:, PACK * first : PACK * (first + count)].bitcast(I32),
                )

        HALF = WIDTH // 2
        REST = WIDTH - K_PASS
        load_rows(sx_sb, state_x, 0, K_PASS)
        load_rows(x_sb, x, 0, K_PASS)
        load_mix()
        load_rows(sx_sb, state_x, K_PASS, REST)
        load_rows(x_sb, x, K_PASS, REST)
        load_rows(den_sb, wkv_den, 0, WIDTH)
        load_planes(wr_planes, W_receptance_scales)
        load_words(wr_words, W_receptance_words, 0, EARLY, (0, 1, 2))
        load_rows(num_sb, wkv_num, 0, HALF)
        load_words(wr_words, W_receptance_words, 0, EARLY, (3,))
        load_words(wr_words, W_receptance_words, 2, 1, range(GROUPS))
        load_rows(num_sb, wkv_num, HALF, HALF)
        load_words(wr_words, W_receptance_words, 3, 1, range(GROUPS))
        load_planes(wo_planes, W_output_scales)
        for g in range(2):
            for c in range(LATE):
                load_words(wo_words, W_output_words, c, 1, (g,))
        load_words(wo_words, W_output_words, 0, LATE, (2,))
        for c in range(LATE):
            load_words(wo_words, W_output_words, c, 1, (GROUPS - 1,))
        load_words(wo_words, W_output_words, LATE, 1, range(GROUPS))

        mix_t = bank(7, [P, PAIR, P], "mix_t")
        for u in range(PAIR):
            nc.tensor.transpose(mix_t[:, u, :], mix_rows[:].bitcast(F32)[:, u::PAIR], ident[:])
        mix_pairs = mix_t[:].bitcast(BF16).rearrange("p u (r e) -> p r u e", e=PAIR)[:, 0:GROUPS]
        nc.vector.tensor_copy(out=mix[:].rearrange("p (g u e) -> p g u e", u=PAIR, e=PAIR), in_=mix_pairs)
        nc.vector.tensor_scalar(
            out=one_minus_mix[:].rearrange("p (g u e) -> p g u e", u=PAIR, e=PAIR),
            in0=mix_pairs,
            scalar1=-1.0,
            scalar2=1.0,
            op0=ALU.mult,
            op1=ALU.add,
        )

        def transpose_pass(src, g, rows, b, name):
            t_bank = bank(b, [P, PAIR, len(rows) * P], name)
            for i, r in enumerate(rows):
                words = src[:, r, :].bitcast(F32)
                for u in range(PAIR):
                    nc.tensor.transpose(
                        t_bank[:, u, i * P : (i + 1) * P],
                        words[:, WORDS_PASS * g + u : WORDS_PASS * (g + 1) : PAIR],
                        ident[:],
                    )
            return t_bank

        def halves_of(t_bank):
            return t_bank[:].bitcast(BF16).rearrange("p u (r e) -> p u r e", e=PAIR)

        BOTH = tuple(range(ROW_TILES))

        sx_t_of = {}
        x_t_of = {}
        kept_of = {}
        mixed_of = {}
        grouped_of = {}

        def turn_x(g):
            sx_t_of[g] = transpose_pass(sx_sb, g, BOTH, 2 * g, "sx_t")
            x_t_of[g] = transpose_pass(x_sb, g, BOTH, 2 * g + 1, "x_t")

        def keep_part(g):
            kept = work.tile([P, PACK, ROWS], F32, name="kept", bufs=GROUPS, align_bytes=256)
            kept_of[g] = kept
            for t in range(PACK):
                u, e = divmod(t, PAIR)
                col = PACK * g + t
                nc.scalar.activation(
                    out=kept[:, t, :],
                    in_=halves_of(sx_t_of[g])[:, u, :, e],
                    func=ACT.Copy,
                    scale=one_minus_mix[:, col : col + 1],
                )

        def mix_part(g, ts):
            if g not in mixed_of:
                mixed_of[g] = work.tile([P, PACK, ROWS], BF16, name="mixed", align_bytes=256)
            for t in ts:
                u, e = divmod(t, PAIR)
                col = PACK * g + t
                nc.vector.scalar_tensor_tensor(
                    out=mixed_of[g][:, t, :],
                    in0=halves_of(x_t_of[g])[:, u, :, e],
                    scalar=mix[:, col : col + 1],
                    in1=kept_of[g][:, t, :],
                    op0=ALU.mult,
                    op1=ALU.add,
                )

        def group_planes(mixed, first, count):
            grouped = work.tile([P, count, PACK], BF16, name="xr_grouped%d" % count, align_bytes=256)
            nc.vector.tensor_copy(
                out=grouped[:].rearrange("p (c i) t -> p c t i", i=4),
                in_=mixed[:, :, first : first + count].rearrange("p t (c i) -> p c t i", i=4),
            )
            return grouped

        def quantise(grouped, codes, scales, g, first, count):
            nc.vector.quantize_mx(
                out=codes[:, g, first : first + count].bitcast(FP8X4),
                scales=scales[:, g, first : first + count],
                in_=grouped[:].rearrange("p r t -> p (r t)"),
            )

        def accumulators(name, b0):
            return [bank(b0 + r, [P, N_TILE], "%s%d" % (name, r)) for r in range(ROW_TILES)]

        def product(acc, codes, scales, w_words, w_planes, c, g, rows=BOTH, first=None, count=N_TILE):
            if first is None:
                first = c * N_TILE
            for r in rows:
                nc.tensor.matmul_mx(
                    out=acc[r][:, 0:count],
                    lhsT=codes[:, g, r * P : (r + 1) * P].bitcast(FP8X4),
                    lhsT_scale=scales[:, g, r * P : (r + 1) * P],
                    rhs=w_words[:, g, first : first + count].bitcast(FP8X4),
                    rhs_scale=w_planes[PACK * g : P, first : first + count],
                    start=(g == 0),
                    stop=(g == GROUPS - 1),
                )

        def first_product(z, c, g):
            product(z, xr_codes, xr_scales, wr_words, wr_planes, c, g)

        def second_product(y, c, g, rows=BOTH, first=None, count=N_TILE):
            product(y, h_codes, h_scales, wo_words, wo_planes, c, g, rows, first, count)

        def gate_root(c):
            cols = slice(c * N_TILE, (c + 1) * N_TILE)
            nc.scalar.activation(
                out=gate[:, :, cols], in_=den_sb[:, :, cols], func=ACT.Abs_reciprocal_sqrt, scale=6.0
            )

        def gate_square(c):
            cols = slice(c * N_TILE, (c + 1) * N_TILE)
            nc.scalar.activation(out=gate[:, :, cols], in_=gate[:, :, cols], func=ACT.Square)

        def gate_times_num(c):
            cols = slice(c * N_TILE, (c + 1) * N_TILE)
            nc.vector.tensor_mul(out=gate[:, :, cols], in0=num_sb[:, :, cols], in1=gate[:, :, cols])

        ramp_of = {}

        def ramp_up(z, c, rows=BOTH):
            for r in rows:
                ramp = work.tile([P, N_TILE], F32, name="ramp", bufs=RAMPS, align_bytes=256)
                nc.scalar.activation(out=ramp[:], in_=z[r][:], func=ACT.Relu, bias=3.0)
                ramp_of[(c, r)] = ramp

        def gated(c, rows=BOTH):
            cols = slice(c * N_TILE, (c + 1) * N_TILE)
            for r in rows:
                nc.vector.scalar_tensor_tensor(
                    out=h_sb[:, r, cols],
                    in0=ramp_of[(c, r)][:],
                    scalar=6.0,
                    in1=gate[:, r, cols],
                    op0=ALU.min,
                    op1=ALU.mult,
                )

        def turn_h(g, rows, b):
            return transpose_pass(h_sb, g, rows, b, "h_t")

        def group_h(h_t, rows, engine_copy):
            grouped = work.tile([P, len(rows) * P, PACK], BF16, name="h_grouped%d" % len(rows), align_bytes=256)
            engine_copy(
                out=grouped[:].rearrange("p r t -> p (r t)").bitcast(F32).rearrange("p (r u) -> p r u", u=PAIR),
                in_=h_t[:].rearrange("p u r -> p r u"),
            )
            return grouped

        out_rows = out.rearrange("(r p) e -> p r e", p=P)

        def leave(y, c, first=None, count=N_TILE):
            if first is None:
                first = c * N_TILE
            cols = slice(first, first + count)
            nc.scalar.copy(out=out_sb[:, 0, cols], in_=y[0][:, 0:count])
            nc.vector.tensor_copy(out=out_sb[:, 1, cols], in_=y[1][:, 0:count])
            for r in range(ROW_TILES):
                nc.sync.dma_start(out=out_rows[:, r, cols], in_=out_sb[:, r, cols])

        z_of = {}
        y_of = {}
        hq = {}
        ht = {}
        for g in range(GROUPS):
            turn_x(g)
            keep_part(g)
        gate_root(0)
        gate_root(1)
        gate_square(0)
        gate_square(1)
        gate_root(2)
        gate_root(3)
        mix_part(0, range(PACK))
        for g in range(GROUPS - 1):
            mix_part(g + 1, (0, 1))
            grouped_of[g] = group_planes(mixed_of[g], 0, ROWS)
            mix_part(g + 1, (2, 3))
            quantise(grouped_of[g], xr_codes, xr_scales, g, 0, ROWS)
            for c in range(EARLY):
                if g == 0:
                    z_of[c] = accumulators("z", 2 * c)
                first_product(z_of[c], c, g)
        last = GROUPS - 1
        for r in range(ROW_TILES):
            grouped_of[(last, r)] = group_planes(mixed_of[last], r * P, P)
        for r in range(ROW_TILES):
            quantise(grouped_of[(last, r)], xr_codes, xr_scales, last, r * P, P)
        for c in range(EARLY):
            first_product(z_of[c], c, last)
        gate_times_num(0)
        gate_times_num(1)
        ramp_up(z_of[0], 0)
        gated(0)
        ramp_up(z_of[1], 1)
        gated(1)
        z_of[2] = accumulators("z", 4)
        for g in range(GROUPS):
            first_product(z_of[2], 2, g)
        ht[0] = turn_h(0, BOTH, 0)
        ht[1] = turn_h(1, BOTH, 1)
        gate_square(2)
        ramp_up(z_of[2], 2)
        gate_times_num(2)
        gated(2)
        hq[0] = group_h(ht[0], BOTH, nc.scalar.copy)
        hq[1] = group_h(ht[1], BOTH, nc.scalar.copy)
        quantise(hq[0], h_codes, h_scales, 0, 0, ROWS)
        quantise(hq[1], h_codes, h_scales, 1, 0, ROWS)
        z_of[3] = accumulators("z", 6)
        for g in range(GROUPS):
            first_product(z_of[3], 3, g)
        gate_square(3)
        gate_times_num(3)
        ht[2] = turn_h(2, BOTH, 0)
        ramp_up(z_of[3], 3)
        y_of[0] = accumulators("y", 2)
        y_of[1] = accumulators("y", 4)
        for c in range(2):
            second_product(y_of[c], c, 0)
        y_of[2] = accumulators("y", 6)
        second_product(y_of[2], 2, 0)
        gated(3, (0,))
        gated(3, (1,))
        hq[2] = group_h(ht[2], BOTH, nc.scalar.copy)
        quantise(hq[2], h_codes, h_scales, 2, 0, ROWS)
        for c in range(EARLY):
            second_product(y_of[c], c, 1)
        ht[3] = turn_h(3, (0,), 1)
        ht[4] = turn_h(3, (1,), 0)
        hq[3] = group_h(ht[3], (0,), nc.scalar.copy)
        hq[4] = group_h(ht[4], (1,), nc.scalar.copy)
        quantise(hq[3], h_codes, h_scales, 3, 0, P)
        quantise(hq[4], h_codes, h_scales, 3, P, P)
        second_product(y_of[2], 2, 1)
        for c in range(LATE):
            second_product(y_of[c], c, 2)
            second_product(y_of[c], c, 3)
            leave(y_of[c], c)
        for half in range(2):
            y_last = accumulators("y", 2 * half)
            first = LATE * N_TILE + half * (N_TILE // 2)
            for g in range(GROUPS):
                second_product(y_last, LATE, g, BOTH, first, N_TILE // 2)
            leave(y_last, LATE, first, N_TILE // 2)
